import numpy as np
import ml_dtypes


def mxq(x, axis, fmt="e4m3"):
    dtype, down = {"e4m3": (ml_dtypes.float8_e4m3fn, 7), "e5m2": (ml_dtypes.float8_e5m2, 14)}[fmt]
    v = np.moveaxis(np.asarray(x, np.float32).astype(ml_dtypes.bfloat16).astype(np.float64), axis, -1)
    blocks = v.reshape(v.shape[:-1] + (-1, 32))
    amax = np.abs(blocks).max(-1, keepdims=True)
    byte = np.maximum(np.where(amax > 0, np.frexp(amax)[1] - 1 + 127, 0) - down, 1)
    scale = np.exp2(byte - 127.0)
    codes = (blocks / scale).astype(np.float32).astype(dtype).astype(np.float64)
    return np.moveaxis((codes * scale).reshape(v.shape), -1, axis)


WIDE = False


def mx_kscale(k):
    if not WIDE:
        return np.ones(k)
    levels = np.array([10, -10, 5, -5, 0])
    a = np.random.permutation(np.resize(levels, k // 512 * 4)).reshape(k // 512, 4)
    idx = np.arange(k)
    return np.exp2(a[idx // 512, idx % 128 // 32])


BF16 = ml_dtypes.bfloat16


def bf(x):
    return np.asarray(x, np.float32).astype(BF16)


def f64(x):
    return np.asarray(x).astype(np.float64)


E2M1 = np.array([0.0, 0.5, 1.0, 1.5, 2.0, 3.0, 4.0, 6.0, -0.0, -0.5, -1.0, -1.5, -2.0, -3.0, -4.0, -6.0])


def pack_weight(w, fmt):
    k, n = w.shape
    w = f64(bf(w)).reshape(k // 32, 32, n)
    amax = np.abs(w).max(1)
    if fmt == "e4m3":
        byte = np.frexp(amax)[1] - 1 + 127 - 7
    else:
        mant, ex = np.frexp(amax / 6.0)
        byte = np.where(mant > 0.5, ex, ex - 1) + 127
    byte = np.clip(np.where(amax > 0, byte, 1), 1, 254)
    scaled = (w * np.exp2(127.0 - byte)[:, None, :]).reshape(k, n).astype(np.float32)
    by_word = np.ascontiguousarray(scaled.reshape(k // 512, 128, 4, n).transpose(0, 1, 3, 2))
    if fmt == "e4m3":
        words = by_word.astype(ml_dtypes.float8_e4m3fn).view(np.uint8)
    else:
        c = by_word.astype(ml_dtypes.float4_e2m1fn).view(np.uint8) & 0xF
        words = c[..., 0::2] | (c[..., 1::2] << 4)
    return np.ascontiguousarray(words), np.ascontiguousarray(byte.astype(np.uint8).reshape(k // 512, 16, n))


def unpack_weight(words, scales, fmt):
    g, p, n, _ = words.shape
    if fmt == "e4m3":
        vals = np.ascontiguousarray(words).view(ml_dtypes.float8_e4m3fn).astype(np.float64)
    else:
        nib = np.empty((g, p, n, 4), np.uint8)
        nib[..., 0::2] = words & 0xF
        nib[..., 1::2] = words >> 4
        vals = E2M1[nib]
    vals = vals * np.repeat(np.exp2(scales.astype(np.float64) - 127.0), 8, axis=1)[..., None]
    return vals.transpose(0, 1, 3, 2).reshape(g * 512, n)


B, U, I = 512, 1024, 512
K = U + I
FMT = "e4m3"


def sigmoid(v):
    return 1.0 / (1.0 + np.exp(-v))


def setup_inputs():
    s = mx_kscale(K)
    inputs = bf(np.random.standard_normal((B, I)) * s[U:])
    h_tm1 = bf(np.random.standard_normal((B, U)) * s[:U])
    c_tm1 = bf(np.random.standard_normal((B, U)))
    words, scales = pack_weight(np.random.standard_normal((K, 4 * U)) / np.sqrt(K) / s[:, None], FMT)
    return {"inputs": inputs,
            "h_tm1": h_tm1,
            "c_tm1": c_tm1,
            "kernel_words": words,
            "kernel_scales": scales}


def reference(inputs, h_tm1, c_tm1, kernel_words, kernel_scales):
    a = np.concatenate([f64(h_tm1), f64(inputs)], axis=-1)
    z = mxq(a, 1, "e4m3") @ unpack_weight(kernel_words, kernel_scales, FMT)
    z0, z1, z2, z3 = np.split(z, 4, axis=-1)
    i = sigmoid(z0)
    f = sigmoid(z1)
    c_tilde = np.tanh(z2)
    o = sigmoid(z3)
    c = f * f64(c_tm1) + i * c_tilde
    h = o * np.tanh(c)
    return (h, c)

@@ -1,0 +1,137 @@
+from contextlib import ExitStack
+
+import concourse.mybir as mybir
+from concourse.masks import make_identity
+
+F32 = mybir.dt.float32
+BF16 = mybir.dt.bfloat16
+I32 = mybir.dt.int32
+U32 = mybir.dt.uint32
+U8 = mybir.dt.uint8
+FP8X4 = mybir.dt.float8_e4m3fn_x4
+SIGMOID = mybir.ActivationFunctionType.Sigmoid
+TANH = mybir.ActivationFunctionType.Tanh
+
+P = 128
+PACK = 4
+K_PASS = P * PACK
+BATCH, UNITS, FEATURES = 512, 1024, 512
+PASSES = (UNITS + FEATURES) // K_PASS
+ROW_SETS = BATCH // P
+CHUNK = 512
+CHUNKS = UNITS // CHUNK
+SCALE_ROWS = 4
+QUADRANTS = 4
+Z_I, Z_F, Z_C_TILDE, Z_O = 0, UNITS, 2 * UNITS, 3 * UNITS
+GATE_ORDER = (Z_I, Z_C_TILDE, Z_F, Z_O)
+
+FLOPS = 2 * BATCH * (UNITS + FEATURES) * 4 * UNITS
+
+
+def tile_customlstmcell_kernel(tc, inputs, h_tm1, c_tm1, kernel_words, kernel_scales, out_0, out_1):
+    nc = tc.nc
+    with ExitStack() as ctx:
+        keep = ctx.enter_context(tc.tile_pool(name="keep", bufs=1))
+        work = ctx.enter_context(tc.tile_pool(name="work", bufs=ROW_SETS))
+        psum = ctx.enter_context(tc.psum_pool(name="psum", bufs=8))
+
+        identity = keep.tile([P, P], F32)
+        make_identity(nc, identity[:])
+        w_scales = keep.tile([P, 4 * UNITS], U8, align_bytes=64)
+        nc.vector.memset(w_scales[:].bitcast(I32), 0)
+
+        act_raw = []
+        for g in range(PASSES):
+            k_lo = g * K_PASS
+            source = h_tm1[:, k_lo : k_lo + K_PASS] if k_lo < UNITS else inputs[:, k_lo - UNITS : k_lo - UNITS + K_PASS]
+            raw = keep.tile([P, ROW_SETS, K_PASS], BF16, name="act_raw%d" % g)
+            nc.sync.dma_start(out=raw[:], in_=source.rearrange("(p m) k -> p m k", m=ROW_SETS))
+            act_raw.append(raw)
+
+        scale_words = kernel_scales.bitcast(I32)
+        for quadrant in range(QUADRANTS):
+            first = 32 * quadrant
+            nc.sync.dma_start(
+                out=w_scales[first : first + PASSES * SCALE_ROWS, :].bitcast(I32),
+                in_=scale_words[:, SCALE_ROWS * quadrant : SCALE_ROWS * (quadrant + 1), :],
+            )
+
+        c_prev = keep.tile([P, ROW_SETS, UNITS], BF16)
+        words_by_partition = kernel_words.rearrange("g q n t -> q g (n t)")
+        w_words = {}
+        for j in range(CHUNKS):
+            for z_lo in GATE_ORDER:
+                n_lo = z_lo + j * CHUNK
+                piece = keep.tile([P, PASSES, CHUNK], U32, align_bytes=64, name="w_words_%d_%d" % (j, z_lo))
+                nc.sync.dma_start(
+                    out=piece[:].bitcast(I32),
+                    in_=words_by_partition[:, :, PACK * n_lo : PACK * (n_lo + CHUNK)].bitcast(I32),
+                )
+                w_words[(j, z_lo)] = piece
+                if j == 0 and z_lo == Z_C_TILDE:
+                    nc.sync.dma_start(out=c_prev[:], in_=c_tm1.rearrange("(p m) u -> p m u", m=ROW_SETS))
+
+        act_codes = keep.tile([P, PASSES, ROW_SETS, P], U32, align_bytes=64)
+        act_scales = keep.tile([P, PASSES, ROW_SETS, P], U8, align_bytes=64)
+        for g in range(PASSES):
+            pairs_of_k = act_raw[g][:].bitcast(F32)
+            grouped = keep.tile([P, ROW_SETS, P, PACK], BF16, align_bytes=64, name="grouped%d" % g)
+            for m_lo in range(0, ROW_SETS, 2):
+                two_sets = slice(m_lo, m_lo + 2)
+                flipped = psum.tile([P, 2, 2, P], F32, tag="bank")
+                for s in range(2):
+                    for u in range(2):
+                        nc.tensor.transpose(flipped[:, s, u, :], pairs_of_k[:, m_lo + s, u : K_PASS // 2 : 2], identity[:])
+                nc.scalar.copy(
+                    out=grouped[:, two_sets, :, :].bitcast(F32),
+                    in_=flipped[:].rearrange("q s u r -> q s r u"),
+                )
+                nc.vector.quantize_mx(
+                    out=act_codes[:, g, two_sets, :].rearrange("q s r -> q (s r)").bitcast(FP8X4),
+                    scales=act_scales[:, g, two_sets, :].rearrange("q s r -> q (s r)"),
+                    in_=grouped[:, two_sets, :, :].rearrange("q s r t -> q (s r t)"),
+                )
+
+        def gate(j, z_lo, m, func, tag):
+            n_lo = z_lo + j * CHUNK
+            acc = psum.tile([P, CHUNK], F32, tag="bank")
+            for g in range(PASSES):
+                nc.tensor.matmul_mx(
+                    out=acc[:],
+                    lhsT=act_codes[:, g, m, :].bitcast(FP8X4),
+                    lhsT_scale=act_scales[:, g, m, :],
+                    rhs=w_words[(j, z_lo)][:, g, :].bitcast(FP8X4),
+                    rhs_scale=w_scales[SCALE_ROWS * g : P, n_lo : n_lo + CHUNK],
+                    start=(g == 0),
+                    stop=(g == PASSES - 1),
+                )
+            value = work.tile([P, CHUNK], F32, tag=tag, name=tag)
+            nc.scalar.activation(out=value[:], in_=acc[:], func=func)
+            return value
+
+        h_out = out_0.rearrange("(p m) u -> p m u", m=ROW_SETS)
+        c_out = out_1.rearrange("(p m) u -> p m u", m=ROW_SETS)
+        for j in range(CHUNKS):
+            units = slice(j * CHUNK, (j + 1) * CHUNK)
+            i_gate = [gate(j, Z_I, m, SIGMOID, "i_gate") for m in range(ROW_SETS)]
+            i_c_tilde = []
+            for m in range(ROW_SETS):
+                c_tilde = gate(j, Z_C_TILDE, m, TANH, "c_tilde")
+                product = work.tile([P, CHUNK], F32, tag="i_c_tilde", name="i_c_tilde")
+                nc.vector.tensor_mul(out=product[:], in0=i_gate[m][:], in1=c_tilde[:])
+                i_c_tilde.append(product)
+            tanh_c = []
+            for m in range(ROW_SETS):
+                f_gate = gate(j, Z_F, m, SIGMOID, "f_gate")
+                c_new = work.tile([P, CHUNK], F32, tag="c_new", name="c_new")
+                nc.vector.tensor_mul(out=c_new[:], in0=f_gate[:], in1=c_prev[:, m, units])
+                nc.vector.tensor_add(out=c_new[:], in0=c_new[:], in1=i_c_tilde[m][:])
+                nc.sync.dma_start(out=c_out[:, m, units], in_=c_new[:])
+                squashed = work.tile([P, CHUNK], F32, tag="tanh_c", name="tanh_c")
+                nc.scalar.activation(out=squashed[:], in_=c_new[:], func=TANH)
+                tanh_c.append(squashed)
+            for m in range(ROW_SETS):
+                o_gate = gate(j, Z_O, m, SIGMOID, "o_gate")
+                h_new = work.tile([P, CHUNK], F32, tag="h_new", name="h_new")
+                nc.vector.tensor_mul(out=h_new[:], in0=o_gate[:], in1=tanh_c[m][:])
+                nc.sync.dma_start(out=h_out[:, m, units], in_=h_new[:])

@@ -48,11 +48,11 @@ def tile_customlstmcell_kernel(tc, inputs, h_tm1, c_tm1, kernel_words, kernel_sc
             nc.sync.dma_start(out=raw[:], in_=source.rearrange("(p m) k -> p m k", m=ROW_SETS))
             act_raw.append(raw)
 
-        scale_words = kernel_scales.bitcast(I32)
+        scale_words = kernel_scales.bitcast(F32)
         for quadrant in range(QUADRANTS):
             first = 32 * quadrant
-            nc.sync.dma_start(
-                out=w_scales[first : first + PASSES * SCALE_ROWS, :].bitcast(I32),
+            nc.gpsimd.dma_start(
+                out=w_scales[first : first + PASSES * SCALE_ROWS, :].bitcast(F32),
                 in_=scale_words[:, SCALE_ROWS * quadrant : SCALE_ROWS * (quadrant + 1), :],
             )
 

@@ -22,8 +22,11 @@ CHUNK = 512
 CHUNKS = UNITS // CHUNK
 SCALE_ROWS = 4
 QUADRANTS = 4
+PSUM_BANKS = 8
 Z_I, Z_F, Z_C_TILDE, Z_O = 0, UNITS, 2 * UNITS, 3 * UNITS
-GATE_ORDER = (Z_I, Z_C_TILDE, Z_F, Z_O)
+CELL_GATES = (Z_I, Z_C_TILDE, Z_F)
+TANH_LAG = 3
+O_WIDTHS = (CHUNK, CHUNK // 2)
 
 FLOPS = 2 * BATCH * (UNITS + FEATURES) * 4 * UNITS
 
@@ -31,107 +34,145 @@ FLOPS = 2 * BATCH * (UNITS + FEATURES) * 4 * UNITS
 def tile_customlstmcell_kernel(tc, inputs, h_tm1, c_tm1, kernel_words, kernel_scales, out_0, out_1):
     nc = tc.nc
     with ExitStack() as ctx:
+        ctx.enter_context(tc.manual_schedule())
         keep = ctx.enter_context(tc.tile_pool(name="keep", bufs=1))
+        stage = ctx.enter_context(tc.tile_pool(name="stage", bufs=3))
         work = ctx.enter_context(tc.tile_pool(name="work", bufs=ROW_SETS))
-        psum = ctx.enter_context(tc.psum_pool(name="psum", bufs=8))
+        results = ctx.enter_context(tc.tile_pool(name="results", bufs=CHUNKS * ROW_SETS))
+        psum = ctx.enter_context(tc.psum_pool(name="psum", bufs=PSUM_BANKS))
 
         identity = keep.tile([P, P], F32)
         make_identity(nc, identity[:])
         w_scales = keep.tile([P, 4 * UNITS], U8, align_bytes=64)
         nc.vector.memset(w_scales[:].bitcast(I32), 0)
 
-        act_raw = []
-        for g in range(PASSES):
-            k_lo = g * K_PASS
-            source = h_tm1[:, k_lo : k_lo + K_PASS] if k_lo < UNITS else inputs[:, k_lo - UNITS : k_lo - UNITS + K_PASS]
-            raw = keep.tile([P, ROW_SETS, K_PASS], BF16, name="act_raw%d" % g)
-            nc.sync.dma_start(out=raw[:], in_=source.rearrange("(p m) k -> p m k", m=ROW_SETS))
-            act_raw.append(raw)
+        h_rows = h_tm1.rearrange("(p m) k -> p m k", m=ROW_SETS)
+        x_rows = inputs.rearrange("(p m) k -> p m k", m=ROW_SETS)
+        h_raw = []
+        x_raw = []
+        for m_lo in range(0, ROW_SETS, 2):
+            h_part = keep.tile([P, 2, UNITS], BF16, name="h_raw%d" % m_lo)
+            nc.sync.dma_start(out=h_part[:], in_=h_rows[:, m_lo : m_lo + 2, :])
+            h_raw.append(h_part)
+            x_part = keep.tile([P, 2, FEATURES], BF16, name="x_raw%d" % m_lo)
+            nc.sync.dma_start(out=x_part[:], in_=x_rows[:, m_lo : m_lo + 2, :])
+            x_raw.append(x_part)
 
-        scale_words = kernel_scales.bitcast(F32)
-        for quadrant in range(QUADRANTS):
-            first = 32 * quadrant
-            nc.gpsimd.dma_start(
-                out=w_scales[first : first + PASSES * SCALE_ROWS, :].bitcast(F32),
-                in_=scale_words[:, SCALE_ROWS * quadrant : SCALE_ROWS * (quadrant + 1), :],
-            )
+        scale_words = kernel_scales.bitcast(I32)
 
-        c_prev = keep.tile([P, ROW_SETS, UNITS], BF16)
+        def load_w_scales(n_lo, n_hi):
+            for quadrant in range(QUADRANTS):
+                first = 32 * quadrant
+                nc.sync.dma_start(
+                    out=w_scales[first : first + PASSES * SCALE_ROWS, n_lo:n_hi].bitcast(I32),
+                    in_=scale_words[:, SCALE_ROWS * quadrant : SCALE_ROWS * (quadrant + 1), n_lo // 4 : n_hi // 4],
+                )
+
         words_by_partition = kernel_words.rearrange("g q n t -> q g (n t)")
         w_words = {}
+
+        def load_w_piece(j, z_lo):
+            n_lo = z_lo + j * CHUNK
+            piece = keep.tile([P, PASSES, CHUNK], U32, align_bytes=64, name="w_words_%d_%d" % (j, z_lo))
+            nc.sync.dma_start(
+                out=piece[:].bitcast(I32),
+                in_=words_by_partition[:, :, PACK * n_lo : PACK * (n_lo + CHUNK)].bitcast(I32),
+            )
+            w_words[(j, z_lo)] = piece
+
+        load_w_scales(Z_I, Z_I + UNITS)
+        load_w_piece(0, Z_I)
+        load_w_scales(Z_I + UNITS, 4 * UNITS)
+        load_w_piece(0, Z_C_TILDE)
+        load_w_piece(0, Z_F)
+        c_prev = keep.tile([P, ROW_SETS, UNITS], BF16)
+        nc.sync.dma_start(out=c_prev[:], in_=c_tm1.rearrange("(p m) u -> p m u", m=ROW_SETS))
+        for z_lo in CELL_GATES:
+            load_w_piece(1, z_lo)
         for j in range(CHUNKS):
-            for z_lo in GATE_ORDER:
-                n_lo = z_lo + j * CHUNK
-                piece = keep.tile([P, PASSES, CHUNK], U32, align_bytes=64, name="w_words_%d_%d" % (j, z_lo))
-                nc.sync.dma_start(
-                    out=piece[:].bitcast(I32),
-                    in_=words_by_partition[:, :, PACK * n_lo : PACK * (n_lo + CHUNK)].bitcast(I32),
-                )
-                w_words[(j, z_lo)] = piece
-                if j == 0 and z_lo == Z_C_TILDE:
-                    nc.sync.dma_start(out=c_prev[:], in_=c_tm1.rearrange("(p m) u -> p m u", m=ROW_SETS))
+            load_w_piece(j, Z_O)
 
         act_codes = keep.tile([P, PASSES, ROW_SETS, P], U32, align_bytes=64)
         act_scales = keep.tile([P, PASSES, ROW_SETS, P], U8, align_bytes=64)
-        for g in range(PASSES):
-            pairs_of_k = act_raw[g][:].bitcast(F32)
-            grouped = keep.tile([P, ROW_SETS, P, PACK], BF16, align_bytes=64, name="grouped%d" % g)
-            for m_lo in range(0, ROW_SETS, 2):
-                two_sets = slice(m_lo, m_lo + 2)
+        for pair in range(ROW_SETS // 2):
+            two_sets = slice(2 * pair, 2 * pair + 2)
+            for g in range(PASSES):
+                k_lo = g * K_PASS
+                part = h_raw[pair][:, :, k_lo : k_lo + K_PASS] if k_lo < UNITS else x_raw[pair][:, :, k_lo - UNITS : k_lo - UNITS + K_PASS]
+                pairs_of_k = part.bitcast(F32)
                 flipped = psum.tile([P, 2, 2, P], F32, tag="bank")
                 for s in range(2):
                     for u in range(2):
-                        nc.tensor.transpose(flipped[:, s, u, :], pairs_of_k[:, m_lo + s, u : K_PASS // 2 : 2], identity[:])
-                nc.scalar.copy(
-                    out=grouped[:, two_sets, :, :].bitcast(F32),
-                    in_=flipped[:].rearrange("q s u r -> q s r u"),
-                )
+                        nc.tensor.transpose(flipped[:, s, u, :], pairs_of_k[:, s, u : K_PASS // 2 : 2], identity[:])
+                grouped = stage.tile([P, 2, P, PACK], BF16, align_bytes=64)
+                nc.scalar.copy(out=grouped[:].bitcast(F32), in_=flipped[:].rearrange("q s u r -> q s r u"))
                 nc.vector.quantize_mx(
                     out=act_codes[:, g, two_sets, :].rearrange("q s r -> q (s r)").bitcast(FP8X4),
                     scales=act_scales[:, g, two_sets, :].rearrange("q s r -> q (s r)"),
-                    in_=grouped[:, two_sets, :, :].rearrange("q s r t -> q (s r t)"),
+                    in_=grouped[:].rearrange("q s r t -> q (s r t)"),
                 )
 
-        def gate(j, z_lo, m, func, tag):
-            n_lo = z_lo + j * CHUNK
-            acc = psum.tile([P, CHUNK], F32, tag="bank")
+        def gate(j, z_lo, m, col_lo, width, func, tag):
+            n_lo = z_lo + j * CHUNK + col_lo
+            acc = psum.tile([P, width], F32, tag="bank")
             for g in range(PASSES):
                 nc.tensor.matmul_mx(
                     out=acc[:],
                     lhsT=act_codes[:, g, m, :].bitcast(FP8X4),
                     lhsT_scale=act_scales[:, g, m, :],
-                    rhs=w_words[(j, z_lo)][:, g, :].bitcast(FP8X4),
-                    rhs_scale=w_scales[SCALE_ROWS * g : P, n_lo : n_lo + CHUNK],
+                    rhs=w_words[(j, z_lo)][:, g, col_lo : col_lo + width].bitcast(FP8X4),
+                    rhs_scale=w_scales[SCALE_ROWS * g : P, n_lo : n_lo + width],
                     start=(g == 0),
                     stop=(g == PASSES - 1),
                 )
-            value = work.tile([P, CHUNK], F32, tag=tag, name=tag)
+            value = work.tile([P, width], F32, tag=tag, name=tag)
             nc.scalar.activation(out=value[:], in_=acc[:], func=func)
             return value
+
+        c_new = {}
+        tanh_c = {}
+
+        def squash_c(j, m):
+            squashed = keep.tile([P, CHUNK], F32, name="tanh_c_%d_%d" % (j, m))
+            nc.scalar.activation(out=squashed[:], in_=c_new[(j, m)][:], func=TANH)
+            tanh_c[(j, m)] = squashed
+
+        def squash_c_left_over(j, m):
+            if m < TANH_LAG:
+                squash_c(j, ROW_SETS - TANH_LAG + m)
 
         h_out = out_0.rearrange("(p m) u -> p m u", m=ROW_SETS)
         c_out = out_1.rearrange("(p m) u -> p m u", m=ROW_SETS)
         for j in range(CHUNKS):
             units = slice(j * CHUNK, (j + 1) * CHUNK)
-            i_gate = [gate(j, Z_I, m, SIGMOID, "i_gate") for m in range(ROW_SETS)]
+            i_gate = []
+            for m in range(ROW_SETS):
+                i_gate.append(gate(j, Z_I, m, 0, CHUNK, SIGMOID, "i_gate"))
+                if j > 0:
+                    squash_c_left_over(j - 1, m)
             i_c_tilde = []
             for m in range(ROW_SETS):
-                c_tilde = gate(j, Z_C_TILDE, m, TANH, "c_tilde")
+                c_tilde = gate(j, Z_C_TILDE, m, 0, CHUNK, TANH, "c_tilde")
                 product = work.tile([P, CHUNK], F32, tag="i_c_tilde", name="i_c_tilde")
                 nc.vector.tensor_mul(out=product[:], in0=i_gate[m][:], in1=c_tilde[:])
                 i_c_tilde.append(product)
-            tanh_c = []
             for m in range(ROW_SETS):
-                f_gate = gate(j, Z_F, m, SIGMOID, "f_gate")
-                c_new = work.tile([P, CHUNK], F32, tag="c_new", name="c_new")
-                nc.vector.tensor_mul(out=c_new[:], in0=f_gate[:], in1=c_prev[:, m, units])
-                nc.vector.tensor_add(out=c_new[:], in0=c_new[:], in1=i_c_tilde[m][:])
-                nc.sync.dma_start(out=c_out[:, m, units], in_=c_new[:])
-                squashed = work.tile([P, CHUNK], F32, tag="tanh_c", name="tanh_c")
-                nc.scalar.activation(out=squashed[:], in_=c_new[:], func=TANH)
-                tanh_c.append(squashed)
+                f_gate = gate(j, Z_F, m, 0, CHUNK, SIGMOID, "f_gate")
+                cell = results.tile([P, CHUNK], F32, tag="c_new", name="c_new")
+                nc.vector.tensor_mul(out=cell[:], in0=f_gate[:], in1=c_prev[:, m, units])
+                nc.vector.tensor_add(out=cell[:], in0=cell[:], in1=i_c_tilde[m][:])
+                nc.sync.dma_start(out=c_out[:, m, units], in_=cell[:])
+                c_new[(j, m)] = cell
+                if m >= TANH_LAG:
+                    squash_c(j, m - TANH_LAG)
+        for j in range(CHUNKS):
+            width = O_WIDTHS[j]
             for m in range(ROW_SETS):
-                o_gate = gate(j, Z_O, m, SIGMOID, "o_gate")
-                h_new = work.tile([P, CHUNK], F32, tag="h_new", name="h_new")
-                nc.vector.tensor_mul(out=h_new[:], in0=o_gate[:], in1=tanh_c[m][:])
-                nc.sync.dma_start(out=h_out[:, m, units], in_=h_new[:])
+                h_new = results.tile([P, CHUNK], F32, tag="h_new", name="h_new")
+                for col_lo in range(0, CHUNK, width):
+                    cols = slice(col_lo, col_lo + width)
+                    o_gate = gate(j, Z_O, m, col_lo, width, SIGMOID, "o_gate")
+                    nc.vector.tensor_mul(out=h_new[:, cols], in0=o_gate[:], in1=tanh_c[(j, m)][:, cols])
+                    nc.sync.dma_start(out=h_out[:, m, j * CHUNK + col_lo : j * CHUNK + col_lo + width], in_=h_new[:, cols])
+                if j == 0:
+                    squash_c_left_over(CHUNKS - 1, m)

@@ -26,6 +26,7 @@ PSUM_BANKS = 8
 Z_I, Z_F, Z_C_TILDE, Z_O = 0, UNITS, 2 * UNITS, 3 * UNITS
 CELL_GATES = (Z_I, Z_C_TILDE, Z_F)
 TANH_LAG = 3
+I_WIDTHS = (CHUNK // 2, CHUNK)
 O_WIDTHS = (CHUNK, CHUNK // 2)
 
 FLOPS = 2 * BATCH * (UNITS + FEATURES) * 4 * UNITS
@@ -37,8 +38,7 @@ def tile_customlstmcell_kernel(tc, inputs, h_tm1, c_tm1, kernel_words, kernel_sc
         ctx.enter_context(tc.manual_schedule())
         keep = ctx.enter_context(tc.tile_pool(name="keep", bufs=1))
         stage = ctx.enter_context(tc.tile_pool(name="stage", bufs=3))
-        work = ctx.enter_context(tc.tile_pool(name="work", bufs=ROW_SETS))
-        results = ctx.enter_context(tc.tile_pool(name="results", bufs=CHUNKS * ROW_SETS))
+        work = ctx.enter_context(tc.tile_pool(name="work", bufs=CHUNKS * ROW_SETS))
         psum = ctx.enter_context(tc.psum_pool(name="psum", bufs=PSUM_BANKS))
 
         identity = keep.tile([P, P], F32)
@@ -60,37 +60,40 @@ def tile_customlstmcell_kernel(tc, inputs, h_tm1, c_tm1, kernel_words, kernel_sc
 
         scale_words = kernel_scales.bitcast(I32)
 
-        def load_w_scales(n_lo, n_hi):
+        def load_w_scales(z_lo):
             for quadrant in range(QUADRANTS):
                 first = 32 * quadrant
                 nc.sync.dma_start(
-                    out=w_scales[first : first + PASSES * SCALE_ROWS, n_lo:n_hi].bitcast(I32),
-                    in_=scale_words[:, SCALE_ROWS * quadrant : SCALE_ROWS * (quadrant + 1), n_lo // 4 : n_hi // 4],
+                    out=w_scales[first : first + PASSES * SCALE_ROWS, z_lo : z_lo + UNITS].bitcast(I32),
+                    in_=scale_words[:, SCALE_ROWS * quadrant : SCALE_ROWS * (quadrant + 1), z_lo // 4 : (z_lo + UNITS) // 4],
                 )
 
         words_by_partition = kernel_words.rearrange("g q n t -> q g (n t)")
         w_words = {}
 
-        def load_w_piece(j, z_lo):
-            n_lo = z_lo + j * CHUNK
+        def load_w_piece(j, z_lo, width):
             piece = keep.tile([P, PASSES, CHUNK], U32, align_bytes=64, name="w_words_%d_%d" % (j, z_lo))
-            nc.sync.dma_start(
-                out=piece[:].bitcast(I32),
-                in_=words_by_partition[:, :, PACK * n_lo : PACK * (n_lo + CHUNK)].bitcast(I32),
-            )
+            for col_lo in range(0, CHUNK, width):
+                n_lo = z_lo + j * CHUNK + col_lo
+                nc.sync.dma_start(
+                    out=piece[:, :, col_lo : col_lo + width].bitcast(I32),
+                    in_=words_by_partition[:, :, PACK * n_lo : PACK * (n_lo + width)].bitcast(I32),
+                )
             w_words[(j, z_lo)] = piece
 
-        load_w_scales(Z_I, Z_I + UNITS)
-        load_w_piece(0, Z_I)
-        load_w_scales(Z_I + UNITS, 4 * UNITS)
-        load_w_piece(0, Z_C_TILDE)
-        load_w_piece(0, Z_F)
-        c_prev = keep.tile([P, ROW_SETS, UNITS], BF16)
-        nc.sync.dma_start(out=c_prev[:], in_=c_tm1.rearrange("(p m) u -> p m u", m=ROW_SETS))
-        for z_lo in CELL_GATES:
-            load_w_piece(1, z_lo)
+        c_rows = c_tm1.rearrange("(p m) u -> p m u", m=ROW_SETS)
+        c_prev = []
         for j in range(CHUNKS):
-            load_w_piece(j, Z_O)
+            for z_lo in CELL_GATES:
+                if j == 0:
+                    load_w_scales(z_lo)
+                load_w_piece(j, z_lo, I_WIDTHS[j] if z_lo == Z_I else CHUNK)
+            c_part = keep.tile([P, ROW_SETS, CHUNK], BF16, name="c_prev%d" % j)
+            nc.sync.dma_start(out=c_part[:], in_=c_rows[:, :, j * CHUNK : (j + 1) * CHUNK])
+            c_prev.append(c_part)
+        load_w_scales(Z_O)
+        for j in range(CHUNKS):
+            load_w_piece(j, Z_O, CHUNK)
 
         act_codes = keep.tile([P, PASSES, ROW_SETS, P], U32, align_bytes=64)
         act_scales = keep.tile([P, PASSES, ROW_SETS, P], U8, align_bytes=64)
@@ -112,7 +115,7 @@ def tile_customlstmcell_kernel(tc, inputs, h_tm1, c_tm1, kernel_words, kernel_sc
                     in_=grouped[:].rearrange("q s r t -> q (s r t)"),
                 )
 
-        def gate(j, z_lo, m, col_lo, width, func, tag):
+        def gate(value, j, z_lo, m, col_lo, width, func):
             n_lo = z_lo + j * CHUNK + col_lo
             acc = psum.tile([P, width], F32, tag="bank")
             for g in range(PASSES):
@@ -125,9 +128,7 @@ def tile_customlstmcell_kernel(tc, inputs, h_tm1, c_tm1, kernel_words, kernel_sc
                     start=(g == 0),
                     stop=(g == PASSES - 1),
                 )
-            value = work.tile([P, width], F32, tag=tag, name=tag)
-            nc.scalar.activation(out=value[:], in_=acc[:], func=func)
-            return value
+            nc.scalar.activation(out=value, in_=acc[:], func=func)
 
         c_new = {}
         tanh_c = {}
@@ -145,21 +146,25 @@ def tile_customlstmcell_kernel(tc, inputs, h_tm1, c_tm1, kernel_words, kernel_sc
         c_out = out_1.rearrange("(p m) u -> p m u", m=ROW_SETS)
         for j in range(CHUNKS):
             units = slice(j * CHUNK, (j + 1) * CHUNK)
-            i_gate = []
-            for m in range(ROW_SETS):
-                i_gate.append(gate(j, Z_I, m, 0, CHUNK, SIGMOID, "i_gate"))
-                if j > 0:
-                    squash_c_left_over(j - 1, m)
+            i_gate = [work.tile([P, CHUNK], F32, tag="i_gate", name="i_gate") for m in range(ROW_SETS)]
+            width = I_WIDTHS[j]
+            for col_lo in range(0, CHUNK, width):
+                for m in range(ROW_SETS):
+                    gate(i_gate[m][:, col_lo : col_lo + width], j, Z_I, m, col_lo, width, SIGMOID)
+                    if j > 0:
+                        squash_c_left_over(j - 1, m)
             i_c_tilde = []
             for m in range(ROW_SETS):
-                c_tilde = gate(j, Z_C_TILDE, m, 0, CHUNK, TANH, "c_tilde")
+                c_tilde = work.tile([P, CHUNK], F32, tag="c_tilde", name="c_tilde")
+                gate(c_tilde[:], j, Z_C_TILDE, m, 0, CHUNK, TANH)
                 product = work.tile([P, CHUNK], F32, tag="i_c_tilde", name="i_c_tilde")
                 nc.vector.tensor_mul(out=product[:], in0=i_gate[m][:], in1=c_tilde[:])
                 i_c_tilde.append(product)
             for m in range(ROW_SETS):
-                f_gate = gate(j, Z_F, m, 0, CHUNK, SIGMOID, "f_gate")
-                cell = results.tile([P, CHUNK], F32, tag="c_new", name="c_new")
-                nc.vector.tensor_mul(out=cell[:], in0=f_gate[:], in1=c_prev[:, m, units])
+                f_gate = work.tile([P, CHUNK], F32, tag="f_gate", name="f_gate")
+                gate(f_gate[:], j, Z_F, m, 0, CHUNK, SIGMOID)
+                cell = work.tile([P, CHUNK], F32, tag="c_new", name="c_new")
+                nc.vector.tensor_mul(out=cell[:], in0=f_gate[:], in1=c_prev[j][:, m, :])
                 nc.vector.tensor_add(out=cell[:], in0=cell[:], in1=i_c_tilde[m][:])
                 nc.sync.dma_start(out=c_out[:, m, units], in_=cell[:])
                 c_new[(j, m)] = cell
@@ -168,11 +173,12 @@ def tile_customlstmcell_kernel(tc, inputs, h_tm1, c_tm1, kernel_words, kernel_sc
         for j in range(CHUNKS):
             width = O_WIDTHS[j]
             for m in range(ROW_SETS):
-                h_new = results.tile([P, CHUNK], F32, tag="h_new", name="h_new")
+                o_gate = work.tile([P, CHUNK], F32, tag="o_gate", name="o_gate")
+                h_new = work.tile([P, CHUNK], F32, tag="h_new", name="h_new")
                 for col_lo in range(0, CHUNK, width):
                     cols = slice(col_lo, col_lo + width)
-                    o_gate = gate(j, Z_O, m, col_lo, width, SIGMOID, "o_gate")
-                    nc.vector.tensor_mul(out=h_new[:, cols], in0=o_gate[:], in1=tanh_c[(j, m)][:, cols])
+                    gate(o_gate[:, cols], j, Z_O, m, col_lo, width, SIGMOID)
+                    nc.vector.tensor_mul(out=h_new[:, cols], in0=o_gate[:, cols], in1=tanh_c[(j, m)][:, cols])
                     nc.sync.dma_start(out=h_out[:, m, j * CHUNK + col_lo : j * CHUNK + col_lo + width], in_=h_new[:, cols])
                 if j == 0:
                     squash_c_left_over(CHUNKS - 1, m)

@@ -26,7 +26,6 @@ PSUM_BANKS = 8
 Z_I, Z_F, Z_C_TILDE, Z_O = 0, UNITS, 2 * UNITS, 3 * UNITS
 CELL_GATES = (Z_I, Z_C_TILDE, Z_F)
 TANH_LAG = 3
-I_WIDTHS = (CHUNK // 2, CHUNK)
 O_WIDTHS = (CHUNK, CHUNK // 2)
 
 FLOPS = 2 * BATCH * (UNITS + FEATURES) * 4 * UNITS
@@ -60,40 +59,37 @@ def tile_customlstmcell_kernel(tc, inputs, h_tm1, c_tm1, kernel_words, kernel_sc
 
         scale_words = kernel_scales.bitcast(I32)
 
-        def load_w_scales(z_lo):
+        def load_w_scales(n_lo, n_hi):
             for quadrant in range(QUADRANTS):
                 first = 32 * quadrant
                 nc.sync.dma_start(
-                    out=w_scales[first : first + PASSES * SCALE_ROWS, z_lo : z_lo + UNITS].bitcast(I32),
-                    in_=scale_words[:, SCALE_ROWS * quadrant : SCALE_ROWS * (quadrant + 1), z_lo // 4 : (z_lo + UNITS) // 4],
+                    out=w_scales[first : first + PASSES * SCALE_ROWS, n_lo:n_hi].bitcast(I32),
+                    in_=scale_words[:, SCALE_ROWS * quadrant : SCALE_ROWS * (quadrant + 1), n_lo // 4 : n_hi // 4],
                 )
 
         words_by_partition = kernel_words.rearrange("g q n t -> q g (n t)")
         w_words = {}
 
-        def load_w_piece(j, z_lo, width):
+        def load_w_piece(j, z_lo):
+            n_lo = z_lo + j * CHUNK
             piece = keep.tile([P, PASSES, CHUNK], U32, align_bytes=64, name="w_words_%d_%d" % (j, z_lo))
-            for col_lo in range(0, CHUNK, width):
-                n_lo = z_lo + j * CHUNK + col_lo
-                nc.sync.dma_start(
-                    out=piece[:, :, col_lo : col_lo + width].bitcast(I32),
-                    in_=words_by_partition[:, :, PACK * n_lo : PACK * (n_lo + width)].bitcast(I32),
-                )
+            nc.sync.dma_start(
+                out=piece[:].bitcast(I32),
+                in_=words_by_partition[:, :, PACK * n_lo : PACK * (n_lo + CHUNK)].bitcast(I32),
+            )
             w_words[(j, z_lo)] = piece
 
-        c_rows = c_tm1.rearrange("(p m) u -> p m u", m=ROW_SETS)
-        c_prev = []
+        load_w_scales(Z_I, Z_I + UNITS)
+        load_w_piece(0, Z_I)
+        load_w_scales(Z_I + UNITS, 4 * UNITS)
+        load_w_piece(0, Z_C_TILDE)
+        load_w_piece(0, Z_F)
+        c_prev = keep.tile([P, ROW_SETS, UNITS], BF16)
+        nc.sync.dma_start(out=c_prev[:], in_=c_tm1.rearrange("(p m) u -> p m u", m=ROW_SETS))
+        for z_lo in CELL_GATES:
+            load_w_piece(1, z_lo)
         for j in range(CHUNKS):
-            for z_lo in CELL_GATES:
-                if j == 0:
-                    load_w_scales(z_lo)
-                load_w_piece(j, z_lo, I_WIDTHS[j] if z_lo == Z_I else CHUNK)
-            c_part = keep.tile([P, ROW_SETS, CHUNK], BF16, name="c_prev%d" % j)
-            nc.sync.dma_start(out=c_part[:], in_=c_rows[:, :, j * CHUNK : (j + 1) * CHUNK])
-            c_prev.append(c_part)
-        load_w_scales(Z_O)
-        for j in range(CHUNKS):
-            load_w_piece(j, Z_O, CHUNK)
+            load_w_piece(j, Z_O)
 
         act_codes = keep.tile([P, PASSES, ROW_SETS, P], U32, align_bytes=64)
         act_scales = keep.tile([P, PASSES, ROW_SETS, P], U8, align_bytes=64)
@@ -147,12 +143,10 @@ def tile_customlstmcell_kernel(tc, inputs, h_tm1, c_tm1, kernel_words, kernel_sc
         for j in range(CHUNKS):
             units = slice(j * CHUNK, (j + 1) * CHUNK)
             i_gate = [work.tile([P, CHUNK], F32, tag="i_gate", name="i_gate") for m in range(ROW_SETS)]
-            width = I_WIDTHS[j]
-            for col_lo in range(0, CHUNK, width):
-                for m in range(ROW_SETS):
-                    gate(i_gate[m][:, col_lo : col_lo + width], j, Z_I, m, col_lo, width, SIGMOID)
-                    if j > 0:
-                        squash_c_left_over(j - 1, m)
+            for m in range(ROW_SETS):
+                gate(i_gate[m][:], j, Z_I, m, 0, CHUNK, SIGMOID)
+                if j > 0:
+                    squash_c_left_over(j - 1, m)
             i_c_tilde = []
             for m in range(ROW_SETS):
                 c_tilde = work.tile([P, CHUNK], F32, tag="c_tilde", name="c_tilde")
@@ -160,15 +154,18 @@ def tile_customlstmcell_kernel(tc, inputs, h_tm1, c_tm1, kernel_words, kernel_sc
                 product = work.tile([P, CHUNK], F32, tag="i_c_tilde", name="i_c_tilde")
                 nc.vector.tensor_mul(out=product[:], in0=i_gate[m][:], in1=c_tilde[:])
                 i_c_tilde.append(product)
-            for m in range(ROW_SETS):
-                f_gate = work.tile([P, CHUNK], F32, tag="f_gate", name="f_gate")
-                gate(f_gate[:], j, Z_F, m, 0, CHUNK, SIGMOID)
-                cell = work.tile([P, CHUNK], F32, tag="c_new", name="c_new")
-                nc.vector.tensor_mul(out=cell[:], in0=f_gate[:], in1=c_prev[j][:, m, :])
-                nc.vector.tensor_add(out=cell[:], in0=cell[:], in1=i_c_tilde[m][:])
-                nc.sync.dma_start(out=c_out[:, m, units], in_=cell[:])
-                c_new[(j, m)] = cell
-                if m >= TANH_LAG:
+            for m in range(ROW_SETS + 1):
+                if m < ROW_SETS:
+                    f_gate = work.tile([P, CHUNK], F32, tag="f_gate", name="f_gate")
+                    gate(f_gate[:], j, Z_F, m, 0, CHUNK, SIGMOID)
+                    cell = work.tile([P, CHUNK], F32, tag="c_new", name="c_new")
+                    nc.vector.tensor_mul(out=cell[:], in0=f_gate[:], in1=c_prev[:, m, units])
+                    c_new[(j, m)] = cell
+                if m > 0:
+                    cell = c_new[(j, m - 1)]
+                    nc.vector.tensor_add(out=cell[:], in0=cell[:], in1=i_c_tilde[m - 1][:])
+                    nc.sync.dma_start(out=c_out[:, m - 1, units], in_=cell[:])
+                if TANH_LAG <= m < ROW_SETS:
                     squash_c(j, m - TANH_LAG)
         for j in range(CHUNKS):
             width = O_WIDTHS[j]

@@ -24,9 +24,9 @@ SCALE_ROWS = 4
 QUADRANTS = 4
 PSUM_BANKS = 8
 Z_I, Z_F, Z_C_TILDE, Z_O = 0, UNITS, 2 * UNITS, 3 * UNITS
-CELL_GATES = (Z_I, Z_C_TILDE, Z_F)
 TANH_LAG = 3
-O_WIDTHS = (CHUNK, CHUNK // 2)
+HALF = CHUNK // 2
+QUARTER = CHUNK // 4
 
 FLOPS = 2 * BATCH * (UNITS + FEATURES) * 4 * UNITS
 
@@ -36,10 +36,13 @@ def tile_customlstmcell_kernel(tc, inputs, h_tm1, c_tm1, kernel_words, kernel_sc
     with ExitStack() as ctx:
         ctx.enter_context(tc.manual_schedule())
         keep = ctx.enter_context(tc.tile_pool(name="keep", bufs=1))
-        stage = ctx.enter_context(tc.tile_pool(name="stage", bufs=3))
+        stage = ctx.enter_context(tc.tile_pool(name="stage", bufs=6))
         work = ctx.enter_context(tc.tile_pool(name="work", bufs=CHUNKS * ROW_SETS))
         psum = ctx.enter_context(tc.psum_pool(name="psum", bufs=PSUM_BANKS))
 
+        one_column = keep.tile([P, 1], F32)
+        nc.vector.memset(one_column[:], 0.0)
+        nc.scalar.activation(out=one_column[:], in_=one_column[:], func=SIGMOID)
         identity = keep.tile([P, P], F32)
         make_identity(nc, identity[:])
         w_scales = keep.tile([P, 4 * UNITS], U8, align_bytes=64)
@@ -47,15 +50,13 @@ def tile_customlstmcell_kernel(tc, inputs, h_tm1, c_tm1, kernel_words, kernel_sc
 
         h_rows = h_tm1.rearrange("(p m) k -> p m k", m=ROW_SETS)
         x_rows = inputs.rearrange("(p m) k -> p m k", m=ROW_SETS)
+        x_raw = keep.tile([P, ROW_SETS, FEATURES], BF16)
+        nc.sync.dma_start(out=x_raw[:], in_=x_rows)
         h_raw = []
-        x_raw = []
         for m_lo in range(0, ROW_SETS, 2):
             h_part = keep.tile([P, 2, UNITS], BF16, name="h_raw%d" % m_lo)
             nc.sync.dma_start(out=h_part[:], in_=h_rows[:, m_lo : m_lo + 2, :])
             h_raw.append(h_part)
-            x_part = keep.tile([P, 2, FEATURES], BF16, name="x_raw%d" % m_lo)
-            nc.sync.dma_start(out=x_part[:], in_=x_rows[:, m_lo : m_lo + 2, :])
-            x_raw.append(x_part)
 
         scale_words = kernel_scales.bitcast(I32)
 
@@ -70,112 +71,171 @@ def tile_customlstmcell_kernel(tc, inputs, h_tm1, c_tm1, kernel_words, kernel_sc
         words_by_partition = kernel_words.rearrange("g q n t -> q g (n t)")
         w_words = {}
 
-        def load_w_piece(j, z_lo):
-            n_lo = z_lo + j * CHUNK
-            piece = keep.tile([P, PASSES, CHUNK], U32, align_bytes=64, name="w_words_%d_%d" % (j, z_lo))
-            nc.sync.dma_start(
-                out=piece[:].bitcast(I32),
-                in_=words_by_partition[:, :, PACK * n_lo : PACK * (n_lo + CHUNK)].bitcast(I32),
-            )
-            w_words[(j, z_lo)] = piece
+        def load_w_piece(j, z_lo, width=CHUNK):
+            for col_lo in range(0, CHUNK, width):
+                n_lo = z_lo + j * CHUNK + col_lo
+                piece = keep.tile([P, PASSES, width], U32, align_bytes=64, name="w_words_%d_%d_%d" % (j, z_lo, col_lo))
+                nc.sync.dma_start(
+                    out=piece[:].bitcast(I32),
+                    in_=words_by_partition[:, :, PACK * n_lo : PACK * (n_lo + width)].bitcast(I32),
+                )
+                for c in range(col_lo, col_lo + width, QUARTER):
+                    w_words[(j, z_lo, c)] = (piece, c - col_lo)
 
-        load_w_scales(Z_I, Z_I + UNITS)
-        load_w_piece(0, Z_I)
-        load_w_scales(Z_I + UNITS, 4 * UNITS)
-        load_w_piece(0, Z_C_TILDE)
+        c_rows = c_tm1.rearrange("(p m) u -> p m u", m=ROW_SETS)
+        c_prev = []
+
+        def load_c_prev(j):
+            part = keep.tile([P, ROW_SETS, CHUNK], BF16, name="c_prev%d" % j)
+            nc.sync.dma_start(out=part[:], in_=c_rows[:, :, j * CHUNK : (j + 1) * CHUNK])
+            c_prev.append(part)
+
+        load_w_scales(Z_I, Z_F + CHUNK)
+        load_w_piece(0, Z_I, HALF)
         load_w_piece(0, Z_F)
-        c_prev = keep.tile([P, ROW_SETS, UNITS], BF16)
-        nc.sync.dma_start(out=c_prev[:], in_=c_tm1.rearrange("(p m) u -> p m u", m=ROW_SETS))
-        for z_lo in CELL_GATES:
-            load_w_piece(1, z_lo)
+        load_c_prev(0)
+        load_w_scales(Z_F + CHUNK, 4 * UNITS)
+        load_w_piece(0, Z_C_TILDE)
+        load_w_piece(1, Z_I)
+        load_c_prev(1)
+        load_w_piece(1, Z_C_TILDE)
+        load_w_piece(1, Z_F)
         for j in range(CHUNKS):
             load_w_piece(j, Z_O)
 
-        act_codes = keep.tile([P, PASSES, ROW_SETS, P], U32, align_bytes=64)
-        act_scales = keep.tile([P, PASSES, ROW_SETS, P], U8, align_bytes=64)
-        for pair in range(ROW_SETS // 2):
-            two_sets = slice(2 * pair, 2 * pair + 2)
-            for g in range(PASSES):
-                k_lo = g * K_PASS
-                part = h_raw[pair][:, :, k_lo : k_lo + K_PASS] if k_lo < UNITS else x_raw[pair][:, :, k_lo - UNITS : k_lo - UNITS + K_PASS]
-                pairs_of_k = part.bitcast(F32)
-                flipped = psum.tile([P, 2, 2, P], F32, tag="bank")
-                for s in range(2):
-                    for u in range(2):
-                        nc.tensor.transpose(flipped[:, s, u, :], pairs_of_k[:, s, u : K_PASS // 2 : 2], identity[:])
-                grouped = stage.tile([P, 2, P, PACK], BF16, align_bytes=64)
-                nc.scalar.copy(out=grouped[:].bitcast(F32), in_=flipped[:].rearrange("q s u r -> q s r u"))
-                nc.vector.quantize_mx(
-                    out=act_codes[:, g, two_sets, :].rearrange("q s r -> q (s r)").bitcast(FP8X4),
-                    scales=act_scales[:, g, two_sets, :].rearrange("q s r -> q (s r)"),
-                    in_=grouped[:].rearrange("q s r t -> q (s r t)"),
-                )
+        h_codes = keep.tile([P, ROW_SETS, 2, P], U32, align_bytes=64)
+        h_scales = keep.tile([P, ROW_SETS, 2, P], U8, align_bytes=64)
+        x_codes = keep.tile([P, ROW_SETS, P], U32, align_bytes=64)
+        x_scales = keep.tile([P, ROW_SETS, P], U8, align_bytes=64)
+        BANKS = (("x", 0), ("x", 1), ("h", 0), ("h", 1), ("h", 2), ("h", 3))
+        grouped = {}
+
+        def flip(b):
+            kind, n = BANKS[b]
+            if kind == "x":
+                part = x_raw[:, 2 * n : 2 * n + 2, :]
+            else:
+                part = h_raw[n // 2][:, n % 2, :].rearrange("p (g k) -> p g k", g=2)
+            pairs_of_k = part.bitcast(F32)
+            flipped = psum.tile([P, 2, 2, P], F32, tag="bank", name="flipped")
+            for s in range(2):
+                for u in range(2):
+                    nc.tensor.transpose(flipped[:, s, u, :], pairs_of_k[:, s, u : K_PASS // 2 : 2], identity[:])
+            side_by_side = stage.tile([P, 2, P, PACK], BF16, align_bytes=64, name="grouped")
+            if b % 2 == 0:
+                nc.scalar.copy(out=side_by_side[:].bitcast(F32), in_=flipped[:].rearrange("q s u r -> q s r u"))
+            else:
+                nc.vector.tensor_copy(out=side_by_side[:].bitcast(F32), in_=flipped[:].rearrange("q s u r -> q s r u"))
+            grouped[b] = side_by_side
+
+        def quantise(b):
+            kind, n = BANKS[b]
+            if kind == "x":
+                codes, scales = x_codes[:, 2 * n : 2 * n + 2, :], x_scales[:, 2 * n : 2 * n + 2, :]
+            else:
+                codes, scales = h_codes[:, n, :, :], h_scales[:, n, :, :]
+            nc.vector.quantize_mx(
+                out=codes.rearrange("q s r -> q (s r)").bitcast(FP8X4),
+                scales=scales.rearrange("q s r -> q (s r)"),
+                in_=grouped[b][:].rearrange("q s r t -> q (s r t)"),
+            )
+
+        for b in range(len(BANKS)):
+            flip(b)
+            if b > 0:
+                quantise(b - 1)
+        quantise(len(BANKS) - 1)
 
         def gate(value, j, z_lo, m, col_lo, width, func):
             n_lo = z_lo + j * CHUNK + col_lo
-            acc = psum.tile([P, width], F32, tag="bank")
+            acc = psum.tile([P, width], F32, tag="bank", name="acc")
+            piece, piece_lo = w_words[(j, z_lo, col_lo)]
             for g in range(PASSES):
                 nc.tensor.matmul_mx(
                     out=acc[:],
-                    lhsT=act_codes[:, g, m, :].bitcast(FP8X4),
-                    lhsT_scale=act_scales[:, g, m, :],
-                    rhs=w_words[(j, z_lo)][:, g, col_lo : col_lo + width].bitcast(FP8X4),
+                    lhsT=(h_codes[:, m, g, :] if g < 2 else x_codes[:, m, :]).bitcast(FP8X4),
+                    lhsT_scale=(h_scales[:, m, g, :] if g < 2 else x_scales[:, m, :]),
+                    rhs=piece[:, g, piece_lo : piece_lo + width].bitcast(FP8X4),
                     rhs_scale=w_scales[SCALE_ROWS * g : P, n_lo : n_lo + width],
                     start=(g == 0),
                     stop=(g == PASSES - 1),
                 )
             nc.scalar.activation(out=value, in_=acc[:], func=func)
 
+        i_gate = {}
+        i_c_tilde = {}
         c_new = {}
         tanh_c = {}
+        h_out = out_0.rearrange("(p m) u -> p m u", m=ROW_SETS)
+        c_out = out_1.rearrange("(p m) u -> p m u", m=ROW_SETS)
 
         def squash_c(j, m):
             squashed = keep.tile([P, CHUNK], F32, name="tanh_c_%d_%d" % (j, m))
             nc.scalar.activation(out=squashed[:], in_=c_new[(j, m)][:], func=TANH)
             tanh_c[(j, m)] = squashed
 
-        def squash_c_left_over(j, m):
-            if m < TANH_LAG:
-                squash_c(j, ROW_SETS - TANH_LAG + m)
+        def i_gates(j, m, col_lo, width):
+            if (j, m) not in i_gate:
+                i_gate[(j, m)] = work.tile([P, CHUNK], F32, tag="i_gate", name="i_gate")
+            gate(i_gate[(j, m)][:, col_lo : col_lo + width], j, Z_I, m, col_lo, width, SIGMOID)
 
-        h_out = out_0.rearrange("(p m) u -> p m u", m=ROW_SETS)
-        c_out = out_1.rearrange("(p m) u -> p m u", m=ROW_SETS)
-        for j in range(CHUNKS):
-            units = slice(j * CHUNK, (j + 1) * CHUNK)
-            i_gate = [work.tile([P, CHUNK], F32, tag="i_gate", name="i_gate") for m in range(ROW_SETS)]
+        def f_part(j, m):
+            f_gate = work.tile([P, CHUNK], F32, tag="f_gate", name="f_gate")
+            gate(f_gate[:], j, Z_F, m, 0, CHUNK, SIGMOID)
+            cell = work.tile([P, CHUNK], F32, tag="c_new", name="c_new")
+            nc.vector.tensor_mul(out=cell[:], in0=f_gate[:], in1=c_prev[j][:, m, :])
+            c_new[(j, m)] = cell
+
+        def c_tilde_part(j, m):
+            c_tilde = work.tile([P, CHUNK], F32, tag="c_tilde", name="c_tilde")
+            gate(c_tilde[:], j, Z_C_TILDE, m, 0, CHUNK, TANH)
+            product = work.tile([P, CHUNK], F32, tag="i_c_tilde", name="i_c_tilde")
+            nc.vector.tensor_mul(out=product[:], in0=i_gate[(j, m)][:], in1=c_tilde[:])
+            i_c_tilde[(j, m)] = product
+
+        def finish_c(j, m):
+            cell = c_new[(j, m)]
+            nc.vector.tensor_add(out=cell[:], in0=cell[:], in1=i_c_tilde[(j, m)][:])
+            nc.sync.dma_start(out=c_out[:, m, j * CHUNK : (j + 1) * CHUNK], in_=cell[:])
+
+        def o_part(j, m, widths):
+            o_gate = work.tile([P, CHUNK], F32, tag="o_gate", name="o_gate")
+            h_new = work.tile([P, CHUNK], F32, tag="h_new", name="h_new")
+            col_lo = 0
+            for width in widths:
+                cols = slice(col_lo, col_lo + width)
+                gate(o_gate[:, cols], j, Z_O, m, col_lo, width, SIGMOID)
+                nc.vector.tensor_mul(out=h_new[:, cols], in0=o_gate[:, cols], in1=tanh_c[(j, m)][:, cols])
+                nc.sync.dma_start(out=h_out[:, m, j * CHUNK + col_lo : j * CHUNK + col_lo + width], in_=h_new[:, cols])
+                col_lo += width
+
+        for col_lo in range(0, CHUNK, HALF):
             for m in range(ROW_SETS):
-                gate(i_gate[m][:], j, Z_I, m, 0, CHUNK, SIGMOID)
-                if j > 0:
-                    squash_c_left_over(j - 1, m)
-            i_c_tilde = []
-            for m in range(ROW_SETS):
-                c_tilde = work.tile([P, CHUNK], F32, tag="c_tilde", name="c_tilde")
-                gate(c_tilde[:], j, Z_C_TILDE, m, 0, CHUNK, TANH)
-                product = work.tile([P, CHUNK], F32, tag="i_c_tilde", name="i_c_tilde")
-                nc.vector.tensor_mul(out=product[:], in0=i_gate[m][:], in1=c_tilde[:])
-                i_c_tilde.append(product)
-            for m in range(ROW_SETS + 1):
-                if m < ROW_SETS:
-                    f_gate = work.tile([P, CHUNK], F32, tag="f_gate", name="f_gate")
-                    gate(f_gate[:], j, Z_F, m, 0, CHUNK, SIGMOID)
-                    cell = work.tile([P, CHUNK], F32, tag="c_new", name="c_new")
-                    nc.vector.tensor_mul(out=cell[:], in0=f_gate[:], in1=c_prev[:, m, units])
-                    c_new[(j, m)] = cell
-                if m > 0:
-                    cell = c_new[(j, m - 1)]
-                    nc.vector.tensor_add(out=cell[:], in0=cell[:], in1=i_c_tilde[m - 1][:])
-                    nc.sync.dma_start(out=c_out[:, m - 1, units], in_=cell[:])
-                if TANH_LAG <= m < ROW_SETS:
-                    squash_c(j, m - TANH_LAG)
-        for j in range(CHUNKS):
-            width = O_WIDTHS[j]
-            for m in range(ROW_SETS):
-                o_gate = work.tile([P, CHUNK], F32, tag="o_gate", name="o_gate")
-                h_new = work.tile([P, CHUNK], F32, tag="h_new", name="h_new")
-                for col_lo in range(0, CHUNK, width):
-                    cols = slice(col_lo, col_lo + width)
-                    gate(o_gate[:, cols], j, Z_O, m, col_lo, width, SIGMOID)
-                    nc.vector.tensor_mul(out=h_new[:, cols], in0=o_gate[:, cols], in1=tanh_c[(j, m)][:, cols])
-                    nc.sync.dma_start(out=h_out[:, m, j * CHUNK + col_lo : j * CHUNK + col_lo + width], in_=h_new[:, cols])
-                if j == 0:
-                    squash_c_left_over(CHUNKS - 1, m)
+                i_gates(0, m, col_lo, HALF)
+        for m in range(ROW_SETS):
+            f_part(0, m)
+        for m in range(ROW_SETS):
+            c_tilde_part(0, m)
+            if m > 0:
+                finish_c(0, m - 1)
+        finish_c(0, ROW_SETS - 1)
+        squash_c(0, 0)
+        for m in range(ROW_SETS):
+            i_gates(1, m, 0, CHUNK)
+            if m + 1 < ROW_SETS:
+                squash_c(0, m + 1)
+        for m in range(ROW_SETS):
+            c_tilde_part(1, m)
+            if m > 0:
+                finish_c(1, m - 1)
+            f_part(1, m)
+            if m >= 2:
+                squash_c(1, m - 2)
+        finish_c(1, ROW_SETS - 1)
+        for m in range(ROW_SETS):
+            o_part(0, m, (CHUNK,))
+            if m < 2:
+                squash_c(1, m + 2)
+        for m in range(ROW_SETS - 1):
+            o_part(1, m, (CHUNK,))
+        o_part(1, ROW_SETS - 1, (HALF, QUARTER, QUARTER))

@@ -40,13 +40,14 @@ def tile_customlstmcell_kernel(tc, inputs, h_tm1, c_tm1, kernel_words, kernel_sc
         work = ctx.enter_context(tc.tile_pool(name="work", bufs=CHUNKS * ROW_SETS))
         psum = ctx.enter_context(tc.psum_pool(name="psum", bufs=PSUM_BANKS))
 
+        w_scales = keep.tile([P, 4 * UNITS], U8, align_bytes=64)
+        nc.vector.memset(w_scales[:, 0 : Z_F + CHUNK].bitcast(I32), 0)
+        nc.vector.memset(w_scales[:, Z_F + CHUNK : 4 * UNITS].bitcast(I32), 0)
         one_column = keep.tile([P, 1], F32)
         nc.vector.memset(one_column[:], 0.0)
         nc.scalar.activation(out=one_column[:], in_=one_column[:], func=SIGMOID)
         identity = keep.tile([P, P], F32)
         make_identity(nc, identity[:])
-        w_scales = keep.tile([P, 4 * UNITS], U8, align_bytes=64)
-        nc.vector.memset(w_scales[:].bitcast(I32), 0)
 
         h_rows = h_tm1.rearrange("(p m) k -> p m k", m=ROW_SETS)
         x_rows = inputs.rearrange("(p m) k -> p m k", m=ROW_SETS)
@@ -71,8 +72,8 @@ def tile_customlstmcell_kernel(tc, inputs, h_tm1, c_tm1, kernel_words, kernel_sc
         words_by_partition = kernel_words.rearrange("g q n t -> q g (n t)")
         w_words = {}
 
-        def load_w_piece(j, z_lo, width=CHUNK):
-            for col_lo in range(0, CHUNK, width):
+        def load_w_piece(j, z_lo, width=CHUNK, only=None):
+            for col_lo in range(0, CHUNK, width) if only is None else (only,):
                 n_lo = z_lo + j * CHUNK + col_lo
                 piece = keep.tile([P, PASSES, width], U32, align_bytes=64, name="w_words_%d_%d_%d" % (j, z_lo, col_lo))
                 nc.sync.dma_start(
@@ -90,12 +91,13 @@ def tile_customlstmcell_kernel(tc, inputs, h_tm1, c_tm1, kernel_words, kernel_sc
             nc.sync.dma_start(out=part[:], in_=c_rows[:, :, j * CHUNK : (j + 1) * CHUNK])
             c_prev.append(part)
 
+        load_w_piece(0, Z_I, HALF, 0)
         load_w_scales(Z_I, Z_F + CHUNK)
-        load_w_piece(0, Z_I, HALF)
+        load_w_piece(0, Z_I, HALF, HALF)
         load_w_piece(0, Z_F)
-        load_c_prev(0)
         load_w_scales(Z_F + CHUNK, 4 * UNITS)
         load_w_piece(0, Z_C_TILDE)
+        load_c_prev(0)
         load_w_piece(1, Z_I)
         load_c_prev(1)
         load_w_piece(1, Z_C_TILDE)

@@ -27,6 +27,8 @@ Z_I, Z_F, Z_C_TILDE, Z_O = 0, UNITS, 2 * UNITS, 3 * UNITS
 TANH_LAG = 3
 HALF = CHUNK // 2
 QUARTER = CHUNK // 4
+FIRST_TANH_1 = 8
+LAST_WIDTHS = ((CHUNK,), (CHUNK,), (HALF, HALF), (HALF, QUARTER, QUARTER))
 
 FLOPS = 2 * BATCH * (UNITS + FEATURES) * 4 * UNITS
 
@@ -84,12 +86,7 @@ def tile_customlstmcell_kernel(tc, inputs, h_tm1, c_tm1, kernel_words, kernel_sc
                     w_words[(j, z_lo, c)] = (piece, c - col_lo)
 
         c_rows = c_tm1.rearrange("(p m) u -> p m u", m=ROW_SETS)
-        c_prev = []
-
-        def load_c_prev(j):
-            part = keep.tile([P, ROW_SETS, CHUNK], BF16, name="c_prev%d" % j)
-            nc.sync.dma_start(out=part[:], in_=c_rows[:, :, j * CHUNK : (j + 1) * CHUNK])
-            c_prev.append(part)
+        c_prev = keep.tile([P, ROW_SETS, UNITS], BF16)
 
         load_w_piece(0, Z_I, HALF, 0)
         load_w_scales(Z_I, Z_F + CHUNK)
@@ -97,13 +94,15 @@ def tile_customlstmcell_kernel(tc, inputs, h_tm1, c_tm1, kernel_words, kernel_sc
         load_w_piece(0, Z_F)
         load_w_scales(Z_F + CHUNK, 4 * UNITS)
         load_w_piece(0, Z_C_TILDE)
-        load_c_prev(0)
+        nc.sync.dma_start(out=c_prev[:], in_=c_rows)
         load_w_piece(1, Z_I)
-        load_c_prev(1)
         load_w_piece(1, Z_C_TILDE)
         load_w_piece(1, Z_F)
+        o_words = keep.tile([P, PASSES, UNITS], U32, align_bytes=64)
+        nc.sync.dma_start(out=o_words[:].bitcast(I32), in_=words_by_partition[:, :, PACK * Z_O : PACK * (Z_O + UNITS)].bitcast(I32))
         for j in range(CHUNKS):
-            load_w_piece(j, Z_O)
+            for c in range(0, CHUNK, QUARTER):
+                w_words[(j, Z_O, c)] = (o_words, j * CHUNK + c)
 
         h_codes = keep.tile([P, ROW_SETS, 2, P], U32, align_bytes=64)
         h_scales = keep.tile([P, ROW_SETS, 2, P], U8, align_bytes=64)
@@ -185,7 +184,7 @@ def tile_customlstmcell_kernel(tc, inputs, h_tm1, c_tm1, kernel_words, kernel_sc
             f_gate = work.tile([P, CHUNK], F32, tag="f_gate", name="f_gate")
             gate(f_gate[:], j, Z_F, m, 0, CHUNK, SIGMOID)
             cell = work.tile([P, CHUNK], F32, tag="c_new", name="c_new")
-            nc.vector.tensor_mul(out=cell[:], in0=f_gate[:], in1=c_prev[j][:, m, :])
+            nc.vector.tensor_mul(out=cell[:], in0=f_gate[:], in1=c_prev[:, m, j * CHUNK : (j + 1) * CHUNK])
             c_new[(j, m)] = cell
 
         def c_tilde_part(j, m):
@@ -221,23 +220,30 @@ def tile_customlstmcell_kernel(tc, inputs, h_tm1, c_tm1, kernel_words, kernel_sc
             if m > 0:
                 finish_c(0, m - 1)
         finish_c(0, ROW_SETS - 1)
-        squash_c(0, 0)
+        gates_done = [0]
+
+        def gate_done():
+            n = gates_done[0]
+            if n % 2 == 0 and n // 2 < ROW_SETS:
+                squash_c(0, n // 2)
+            if n >= FIRST_TANH_1 and (n - FIRST_TANH_1) % 3 == 0 and (n - FIRST_TANH_1) // 3 < ROW_SETS:
+                squash_c(1, (n - FIRST_TANH_1) // 3)
+            gates_done[0] = n + 1
+
         for m in range(ROW_SETS):
             i_gates(1, m, 0, CHUNK)
-            if m + 1 < ROW_SETS:
-                squash_c(0, m + 1)
+            gate_done()
         for m in range(ROW_SETS):
             c_tilde_part(1, m)
             if m > 0:
                 finish_c(1, m - 1)
+            gate_done()
             f_part(1, m)
-            if m >= 2:
-                squash_c(1, m - 2)
+            gate_done()
         finish_c(1, ROW_SETS - 1)
         for m in range(ROW_SETS):
             o_part(0, m, (CHUNK,))
-            if m < 2:
-                squash_c(1, m + 2)
-        for m in range(ROW_SETS - 1):
-            o_part(1, m, (CHUNK,))
-        o_part(1, ROW_SETS - 1, (HALF, QUARTER, QUARTER))
+            gate_done()
+        for m in range(ROW_SETS):
+            o_part(1, m, LAST_WIDTHS[m])
+            gate_done()

@@ -123,10 +123,10 @@ def tile_customlstmcell_kernel(tc, inputs, h_tm1, c_tm1, kernel_words, kernel_sc
                 for u in range(2):
                     nc.tensor.transpose(flipped[:, s, u, :], pairs_of_k[:, s, u : K_PASS // 2 : 2], identity[:])
             side_by_side = stage.tile([P, 2, P, PACK], BF16, align_bytes=64, name="grouped")
-            if b % 2 == 0:
-                nc.scalar.copy(out=side_by_side[:].bitcast(F32), in_=flipped[:].rearrange("q s u r -> q s r u"))
-            else:
+            if b == 1:
                 nc.vector.tensor_copy(out=side_by_side[:].bitcast(F32), in_=flipped[:].rearrange("q s u r -> q s r u"))
+            else:
+                nc.scalar.copy(out=side_by_side[:].bitcast(F32), in_=flipped[:].rearrange("q s u r -> q s r u"))
             grouped[b] = side_by_side
 
         def quantise(b):

@@ -30,6 +30,7 @@ QUARTER = CHUNK // 4
 FIRST_TANH_1 = 8
 LAST_WIDTHS = ((CHUNK,), (CHUNK,), (HALF, HALF), (HALF, QUARTER, QUARTER))
 
+WARM_UP = 4
 FLOPS = 2 * BATCH * (UNITS + FEATURES) * 4 * UNITS
 
 
@@ -42,6 +43,12 @@ def tile_customlstmcell_kernel(tc, inputs, h_tm1, c_tm1, kernel_words, kernel_sc
         work = ctx.enter_context(tc.tile_pool(name="work", bufs=CHUNKS * ROW_SETS))
         psum = ctx.enter_context(tc.psum_pool(name="psum", bufs=PSUM_BANKS))
 
+        zero_words = keep.tile([P, CHUNK // 2], F32)
+        nc.vector.memset(zero_words[:], 0.0)
+        zeros = zero_words[:].bitcast(BF16)
+        for n in range(WARM_UP):
+            unread = psum.tile([P, CHUNK], F32, tag="bank", name="unread")
+            nc.tensor.matmul(out=unread[:], lhsT=zeros[:, 0:P], rhs=zeros, start=True, stop=True)
         w_scales = keep.tile([P, 4 * UNITS], U8, align_bytes=64)
         nc.vector.memset(w_scales[:, 0 : Z_F + CHUNK].bitcast(I32), 0)
         nc.vector.memset(w_scales[:, Z_F + CHUNK : 4 * UNITS].bitcast(I32), 0)

@@ -46,9 +46,13 @@ def tile_customlstmcell_kernel(tc, inputs, h_tm1, c_tm1, kernel_words, kernel_sc
         zero_words = keep.tile([P, CHUNK // 2], F32)
         nc.vector.memset(zero_words[:], 0.0)
         zeros = zero_words[:].bitcast(BF16)
-        for n in range(WARM_UP):
+
+        def keep_warm():
             unread = psum.tile([P, CHUNK], F32, tag="bank", name="unread")
             nc.tensor.matmul(out=unread[:], lhsT=zeros[:, 0:P], rhs=zeros, start=True, stop=True)
+
+        for n in range(WARM_UP):
+            keep_warm()
         w_scales = keep.tile([P, 4 * UNITS], U8, align_bytes=64)
         nc.vector.memset(w_scales[:, 0 : Z_F + CHUNK].bitcast(I32), 0)
         nc.vector.memset(w_scales[:, Z_F + CHUNK : 4 * UNITS].bitcast(I32), 0)
@@ -150,6 +154,8 @@ def tile_customlstmcell_kernel(tc, inputs, h_tm1, c_tm1, kernel_words, kernel_sc
 
         for b in range(len(BANKS)):
             flip(b)
+            if b in (1, 3):
+                keep_warm()
             if b > 0:
                 quantise(b - 1)
         quantise(len(BANKS) - 1)
@@ -217,9 +223,10 @@ def tile_customlstmcell_kernel(tc, inputs, h_tm1, c_tm1, kernel_words, kernel_sc
                 nc.sync.dma_start(out=h_out[:, m, j * CHUNK + col_lo : j * CHUNK + col_lo + width], in_=h_new[:, cols])
                 col_lo += width
 
-        for col_lo in range(0, CHUNK, HALF):
-            for m in range(ROW_SETS):
-                i_gates(0, m, col_lo, HALF)
+        for rows in (range(0, ROW_SETS - 1), range(ROW_SETS - 1, ROW_SETS)):
+            for col_lo in range(0, CHUNK, HALF):
+                for m in rows:
+                    i_gates(0, m, col_lo, HALF)
         for m in range(ROW_SETS):
             f_part(0, m)
         for m in range(ROW_SETS):

@@ -85,23 +85,24 @@ def tile_customlstmcell_kernel(tc, inputs, h_tm1, c_tm1, kernel_words, kernel_sc
         words_by_partition = kernel_words.rearrange("g q n t -> q g (n t)")
         w_words = {}
 
-        def load_w_piece(j, z_lo, width=CHUNK, only=None):
-            for col_lo in range(0, CHUNK, width) if only is None else (only,):
-                n_lo = z_lo + j * CHUNK + col_lo
-                piece = keep.tile([P, PASSES, width], U32, align_bytes=64, name="w_words_%d_%d_%d" % (j, z_lo, col_lo))
-                nc.sync.dma_start(
-                    out=piece[:].bitcast(I32),
-                    in_=words_by_partition[:, :, PACK * n_lo : PACK * (n_lo + width)].bitcast(I32),
-                )
-                for c in range(col_lo, col_lo + width, QUARTER):
-                    w_words[(j, z_lo, c)] = (piece, c - col_lo)
+        def load_w_piece(j, z_lo, g_lo=0, g_hi=PASSES):
+            n_lo = z_lo + j * CHUNK
+            piece = keep.tile([P, g_hi - g_lo, CHUNK], U32, align_bytes=64, name="w_words_%d_%d_%d" % (j, z_lo, g_lo))
+            nc.sync.dma_start(
+                out=piece[:].bitcast(I32),
+                in_=words_by_partition[:, g_lo:g_hi, PACK * n_lo : PACK * (n_lo + CHUNK)].bitcast(I32),
+            )
+            for g in range(g_lo, g_hi):
+                for c in range(0, CHUNK, QUARTER):
+                    w_words[(j, z_lo, c, g)] = (piece, g - g_lo, c)
 
         c_rows = c_tm1.rearrange("(p m) u -> p m u", m=ROW_SETS)
         c_prev = keep.tile([P, ROW_SETS, UNITS], BF16)
 
-        load_w_piece(0, Z_I, HALF, 0)
+        load_w_piece(0, Z_I, 0, 1)
         load_w_scales(Z_I, Z_F + CHUNK)
-        load_w_piece(0, Z_I, HALF, HALF)
+        load_w_piece(0, Z_I, 1, 2)
+        load_w_piece(0, Z_I, 2, PASSES)
         load_w_piece(0, Z_F)
         load_w_scales(Z_F + CHUNK, 4 * UNITS)
         load_w_piece(0, Z_C_TILDE)
@@ -113,7 +114,8 @@ def tile_customlstmcell_kernel(tc, inputs, h_tm1, c_tm1, kernel_words, kernel_sc
         nc.sync.dma_start(out=o_words[:].bitcast(I32), in_=words_by_partition[:, :, PACK * Z_O : PACK * (Z_O + UNITS)].bitcast(I32))
         for j in range(CHUNKS):
             for c in range(0, CHUNK, QUARTER):
-                w_words[(j, Z_O, c)] = (o_words, j * CHUNK + c)
+                for g in range(PASSES):
+                    w_words[(j, Z_O, c, g)] = (o_words, g, j * CHUNK + c)
 
         h_codes = keep.tile([P, ROW_SETS, 2, P], U32, align_bytes=64)
         h_scales = keep.tile([P, ROW_SETS, 2, P], U8, align_bytes=64)
@@ -160,20 +162,23 @@ def tile_customlstmcell_kernel(tc, inputs, h_tm1, c_tm1, kernel_words, kernel_sc
                 quantise(b - 1)
         quantise(len(BANKS) - 1)
 
-        def gate(value, j, z_lo, m, col_lo, width, func):
+        def mx_passes(acc, j, z_lo, m, col_lo, width, g_lo, g_hi):
             n_lo = z_lo + j * CHUNK + col_lo
-            acc = psum.tile([P, width], F32, tag="bank", name="acc")
-            piece, piece_lo = w_words[(j, z_lo, col_lo)]
-            for g in range(PASSES):
+            for g in range(g_lo, g_hi):
+                piece, at, piece_lo = w_words[(j, z_lo, col_lo, g)]
                 nc.tensor.matmul_mx(
                     out=acc[:],
                     lhsT=(h_codes[:, m, g, :] if g < 2 else x_codes[:, m, :]).bitcast(FP8X4),
                     lhsT_scale=(h_scales[:, m, g, :] if g < 2 else x_scales[:, m, :]),
-                    rhs=piece[:, g, piece_lo : piece_lo + width].bitcast(FP8X4),
+                    rhs=piece[:, at, piece_lo : piece_lo + width].bitcast(FP8X4),
                     rhs_scale=w_scales[SCALE_ROWS * g : P, n_lo : n_lo + width],
                     start=(g == 0),
                     stop=(g == PASSES - 1),
                 )
+
+        def gate(value, j, z_lo, m, col_lo, width, func):
+            acc = psum.tile([P, width], F32, tag="bank", name="acc")
+            mx_passes(acc, j, z_lo, m, col_lo, width, 0, PASSES)
             nc.scalar.activation(out=value, in_=acc[:], func=func)
 
         i_gate = {}
@@ -223,10 +228,17 @@ def tile_customlstmcell_kernel(tc, inputs, h_tm1, c_tm1, kernel_words, kernel_sc
                 nc.sync.dma_start(out=h_out[:, m, j * CHUNK + col_lo : j * CHUNK + col_lo + width], in_=h_new[:, cols])
                 col_lo += width
 
-        for rows in (range(0, ROW_SETS - 1), range(ROW_SETS - 1, ROW_SETS)):
-            for col_lo in range(0, CHUNK, HALF):
-                for m in rows:
-                    i_gates(0, m, col_lo, HALF)
+        opened = {}
+        for m in range(ROW_SETS - 1):
+            opened[m] = psum.tile([P, CHUNK], F32, tag="bank", name="acc")
+            mx_passes(opened[m], 0, Z_I, m, 0, CHUNK, 0, 1)
+        for m in range(ROW_SETS - 1):
+            mx_passes(opened[m], 0, Z_I, m, 0, CHUNK, 1, 2)
+        for m in range(ROW_SETS - 1):
+            mx_passes(opened[m], 0, Z_I, m, 0, CHUNK, 2, PASSES)
+            i_gate[(0, m)] = work.tile([P, CHUNK], F32, tag="i_gate", name="i_gate")
+            nc.scalar.activation(out=i_gate[(0, m)][:], in_=opened[m][:], func=SIGMOID)
+        i_gates(0, ROW_SETS - 1, 0, CHUNK)
         for m in range(ROW_SETS):
             f_part(0, m)
         for m in range(ROW_SETS):

@@ -104,8 +104,8 @@ def tile_customlstmcell_kernel(tc, inputs, h_tm1, c_tm1, kernel_words, kernel_sc
         load_w_piece(0, Z_I, 1, 2)
         load_w_piece(0, Z_I, 2, PASSES)
         load_w_piece(0, Z_F)
-        load_w_scales(Z_F + CHUNK, 4 * UNITS)
         load_w_piece(0, Z_C_TILDE)
+        load_w_scales(Z_F + CHUNK, 4 * UNITS)
         nc.sync.dma_start(out=c_prev[:], in_=c_rows)
         load_w_piece(1, Z_I)
         load_w_piece(1, Z_C_TILDE)

from contextlib import ExitStack

import concourse.mybir as mybir
from concourse.masks import make_identity

F32 = mybir.dt.float32
BF16 = mybir.dt.bfloat16
I32 = mybir.dt.int32
U32 = mybir.dt.uint32
U8 = mybir.dt.uint8
FP8X4 = mybir.dt.float8_e4m3fn_x4
SIGMOID = mybir.ActivationFunctionType.Sigmoid
TANH = mybir.ActivationFunctionType.Tanh

P = 128
PACK = 4
K_PASS = P * PACK
BATCH, UNITS, FEATURES = 512, 1024, 512
PASSES = (UNITS + FEATURES) // K_PASS
ROW_SETS = BATCH // P
CHUNK = 512
CHUNKS = UNITS // CHUNK
SCALE_ROWS = 4
QUADRANTS = 4
PSUM_BANKS = 8
Z_I, Z_F, Z_C_TILDE, Z_O = 0, UNITS, 2 * UNITS, 3 * UNITS
TANH_LAG = 3
HALF = CHUNK // 2
QUARTER = CHUNK // 4
FIRST_TANH_1 = 8
LAST_WIDTHS = ((CHUNK,), (CHUNK,), (HALF, HALF), (HALF, QUARTER, QUARTER))

WARM_UP = 4
FLOPS = 2 * BATCH * (UNITS + FEATURES) * 4 * UNITS


def tile_customlstmcell_kernel(tc, inputs, h_tm1, c_tm1, kernel_words, kernel_scales, out_0, out_1):
    nc = tc.nc
    with ExitStack() as ctx:
        ctx.enter_context(tc.manual_schedule())
        keep = ctx.enter_context(tc.tile_pool(name="keep", bufs=1))
        stage = ctx.enter_context(tc.tile_pool(name="stage", bufs=6))
        work = ctx.enter_context(tc.tile_pool(name="work", bufs=CHUNKS * ROW_SETS))
        psum = ctx.enter_context(tc.psum_pool(name="psum", bufs=PSUM_BANKS))

        zero_words = keep.tile([P, CHUNK // 2], F32)
        nc.vector.memset(zero_words[:], 0.0)
        zeros = zero_words[:].bitcast(BF16)

        def keep_warm():
            unread = psum.tile([P, CHUNK], F32, tag="bank", name="unread")
            nc.tensor.matmul(out=unread[:], lhsT=zeros[:, 0:P], rhs=zeros, start=True, stop=True)

        for n in range(WARM_UP):
            keep_warm()
        w_scales = keep.tile([P, 4 * UNITS], U8, align_bytes=64)
        nc.vector.memset(w_scales[:, 0 : Z_F + CHUNK].bitcast(I32), 0)
        nc.vector.memset(w_scales[:, Z_F + CHUNK : 4 * UNITS].bitcast(I32), 0)
        one_column = keep.tile([P, 1], F32)
        nc.vector.memset(one_column[:], 0.0)
        nc.scalar.activation(out=one_column[:], in_=one_column[:], func=SIGMOID)
        identity = keep.tile([P, P], F32)
        make_identity(nc, identity[:])

        h_rows = h_tm1.rearrange("(p m) k -> p m k", m=ROW_SETS)
        x_rows = inputs.rearrange("(p m) k -> p m k", m=ROW_SETS)
        x_raw = keep.tile([P, ROW_SETS, FEATURES], BF16)
        nc.sync.dma_start(out=x_raw[:], in_=x_rows)
        h_raw = []
        for m_lo in range(0, ROW_SETS, 2):
            h_part = keep.tile([P, 2, UNITS], BF16, name="h_raw%d" % m_lo)
            nc.sync.dma_start(out=h_part[:], in_=h_rows[:, m_lo : m_lo + 2, :])
            h_raw.append(h_part)

        scale_words = kernel_scales.bitcast(I32)

        def load_w_scales(n_lo, n_hi):
            for quadrant in range(QUADRANTS):
                first = 32 * quadrant
                nc.sync.dma_start(
                    out=w_scales[first : first + PASSES * SCALE_ROWS, n_lo:n_hi].bitcast(I32),
                    in_=scale_words[:, SCALE_ROWS * quadrant : SCALE_ROWS * (quadrant + 1), n_lo // 4 : n_hi // 4],
                )

        words_by_partition = kernel_words.rearrange("g q n t -> q g (n t)")
        w_words = {}

        def load_w_piece(j, z_lo, g_lo=0, g_hi=PASSES):
            n_lo = z_lo + j * CHUNK
            piece = keep.tile([P, g_hi - g_lo, CHUNK], U32, align_bytes=64, name="w_words_%d_%d_%d" % (j, z_lo, g_lo))
            nc.sync.dma_start(
                out=piece[:].bitcast(I32),
                in_=words_by_partition[:, g_lo:g_hi, PACK * n_lo : PACK * (n_lo + CHUNK)].bitcast(I32),
            )
            for g in range(g_lo, g_hi):
                for c in range(0, CHUNK, QUARTER):
                    w_words[(j, z_lo, c, g)] = (piece, g - g_lo, c)

        c_rows = c_tm1.rearrange("(p m) u -> p m u", m=ROW_SETS)
        c_prev = keep.tile([P, ROW_SETS, UNITS], BF16)

        load_w_piece(0, Z_I, 0, 1)
        load_w_scales(Z_I, Z_F + CHUNK)
        load_w_piece(0, Z_I, 1, 2)
        load_w_piece(0, Z_I, 2, PASSES)
        load_w_piece(0, Z_F)
        load_w_piece(0, Z_C_TILDE)
        load_w_scales(Z_F + CHUNK, 4 * UNITS)
        nc.sync.dma_start(out=c_prev[:], in_=c_rows)
        load_w_piece(1, Z_I)
        load_w_piece(1, Z_C_TILDE)
        load_w_piece(1, Z_F)
        o_words = keep.tile([P, PASSES, UNITS], U32, align_bytes=64)
        nc.sync.dma_start(out=o_words[:].bitcast(I32), in_=words_by_partition[:, :, PACK * Z_O : PACK * (Z_O + UNITS)].bitcast(I32))
        for j in range(CHUNKS):
            for c in range(0, CHUNK, QUARTER):
                for g in range(PASSES):
                    w_words[(j, Z_O, c, g)] = (o_words, g, j * CHUNK + c)

        h_codes = keep.tile([P, ROW_SETS, 2, P], U32, align_bytes=64)
        h_scales = keep.tile([P, ROW_SETS, 2, P], U8, align_bytes=64)
        x_codes = keep.tile([P, ROW_SETS, P], U32, align_bytes=64)
        x_scales = keep.tile([P, ROW_SETS, P], U8, align_bytes=64)
        BANKS = (("x", 0), ("x", 1), ("h", 0), ("h", 1), ("h", 2), ("h", 3))
        grouped = {}

        def flip(b):
            kind, n = BANKS[b]
            if kind == "x":
                part = x_raw[:, 2 * n : 2 * n + 2, :]
            else:
                part = h_raw[n // 2][:, n % 2, :].rearrange("p (g k) -> p g k", g=2)
            pairs_of_k = part.bitcast(F32)
            flipped = psum.tile([P, 2, 2, P], F32, tag="bank", name="flipped")
            for s in range(2):
                for u in range(2):
                    nc.tensor.transpose(flipped[:, s, u, :], pairs_of_k[:, s, u : K_PASS // 2 : 2], identity[:])
            side_by_side = stage.tile([P, 2, P, PACK], BF16, align_bytes=64, name="grouped")
            if b == 1:
                nc.vector.tensor_copy(out=side_by_side[:].bitcast(F32), in_=flipped[:].rearrange("q s u r -> q s r u"))
            else:
                nc.scalar.copy(out=side_by_side[:].bitcast(F32), in_=flipped[:].rearrange("q s u r -> q s r u"))
            grouped[b] = side_by_side

        def quantise(b):
            kind, n = BANKS[b]
            if kind == "x":
                codes, scales = x_codes[:, 2 * n : 2 * n + 2, :], x_scales[:, 2 * n : 2 * n + 2, :]
            else:
                codes, scales = h_codes[:, n, :, :], h_scales[:, n, :, :]
            nc.vector.quantize_mx(
                out=codes.rearrange("q s r -> q (s r)").bitcast(FP8X4),
                scales=scales.rearrange("q s r -> q (s r)"),
                in_=grouped[b][:].rearrange("q s r t -> q (s r t)"),
            )

        for b in range(len(BANKS)):
            flip(b)
            if b in (1, 3):
                keep_warm()
            if b > 0:
                quantise(b - 1)
        quantise(len(BANKS) - 1)

        def mx_passes(acc, j, z_lo, m, col_lo, width, g_lo, g_hi):
            n_lo = z_lo + j * CHUNK + col_lo
            for g in range(g_lo, g_hi):
                piece, at, piece_lo = w_words[(j, z_lo, col_lo, g)]
                nc.tensor.matmul_mx(
                    out=acc[:],
                    lhsT=(h_codes[:, m, g, :] if g < 2 else x_codes[:, m, :]).bitcast(FP8X4),
                    lhsT_scale=(h_scales[:, m, g, :] if g < 2 else x_scales[:, m, :]),
                    rhs=piece[:, at, piece_lo : piece_lo + width].bitcast(FP8X4),
                    rhs_scale=w_scales[SCALE_ROWS * g : P, n_lo : n_lo + width],
                    start=(g == 0),
                    stop=(g == PASSES - 1),
                )

        def gate(value, j, z_lo, m, col_lo, width, func):
            acc = psum.tile([P, width], F32, tag="bank", name="acc")
            mx_passes(acc, j, z_lo, m, col_lo, width, 0, PASSES)
            nc.scalar.activation(out=value, in_=acc[:], func=func)

        i_gate = {}
        i_c_tilde = {}
        c_new = {}
        tanh_c = {}
        h_out = out_0.rearrange("(p m) u -> p m u", m=ROW_SETS)
        c_out = out_1.rearrange("(p m) u -> p m u", m=ROW_SETS)

        def squash_c(j, m):
            squashed = keep.tile([P, CHUNK], F32, name="tanh_c_%d_%d" % (j, m))
            nc.scalar.activation(out=squashed[:], in_=c_new[(j, m)][:], func=TANH)
            tanh_c[(j, m)] = squashed

        def i_gates(j, m, col_lo, width):
            if (j, m) not in i_gate:
                i_gate[(j, m)] = work.tile([P, CHUNK], F32, tag="i_gate", name="i_gate")
            gate(i_gate[(j, m)][:, col_lo : col_lo + width], j, Z_I, m, col_lo, width, SIGMOID)

        def f_part(j, m):
            f_gate = work.tile([P, CHUNK], F32, tag="f_gate", name="f_gate")
            gate(f_gate[:], j, Z_F, m, 0, CHUNK, SIGMOID)
            cell = work.tile([P, CHUNK], F32, tag="c_new", name="c_new")
            nc.vector.tensor_mul(out=cell[:], in0=f_gate[:], in1=c_prev[:, m, j * CHUNK : (j + 1) * CHUNK])
            c_new[(j, m)] = cell

        def c_tilde_part(j, m):
            c_tilde = work.tile([P, CHUNK], F32, tag="c_tilde", name="c_tilde")
            gate(c_tilde[:], j, Z_C_TILDE, m, 0, CHUNK, TANH)
            product = work.tile([P, CHUNK], F32, tag="i_c_tilde", name="i_c_tilde")
            nc.vector.tensor_mul(out=product[:], in0=i_gate[(j, m)][:], in1=c_tilde[:])
            i_c_tilde[(j, m)] = product

        def finish_c(j, m):
            cell = c_new[(j, m)]
            nc.vector.tensor_add(out=cell[:], in0=cell[:], in1=i_c_tilde[(j, m)][:])
            nc.sync.dma_start(out=c_out[:, m, j * CHUNK : (j + 1) * CHUNK], in_=cell[:])

        def o_part(j, m, widths):
            o_gate = work.tile([P, CHUNK], F32, tag="o_gate", name="o_gate")
            h_new = work.tile([P, CHUNK], F32, tag="h_new", name="h_new")
            col_lo = 0
            for width in widths:
                cols = slice(col_lo, col_lo + width)
                gate(o_gate[:, cols], j, Z_O, m, col_lo, width, SIGMOID)
                nc.vector.tensor_mul(out=h_new[:, cols], in0=o_gate[:, cols], in1=tanh_c[(j, m)][:, cols])
                nc.sync.dma_start(out=h_out[:, m, j * CHUNK + col_lo : j * CHUNK + col_lo + width], in_=h_new[:, cols])
                col_lo += width

        opened = {}
        for m in range(ROW_SETS - 1):
            opened[m] = psum.tile([P, CHUNK], F32, tag="bank", name="acc")
            mx_passes(opened[m], 0, Z_I, m, 0, CHUNK, 0, 1)
        for m in range(ROW_SETS - 1):
            mx_passes(opened[m], 0, Z_I, m, 0, CHUNK, 1, 2)
        for m in range(ROW_SETS - 1):
            mx_passes(opened[m], 0, Z_I, m, 0, CHUNK, 2, PASSES)
            i_gate[(0, m)] = work.tile([P, CHUNK], F32, tag="i_gate", name="i_gate")
            nc.scalar.activation(out=i_gate[(0, m)][:], in_=opened[m][:], func=SIGMOID)
        i_gates(0, ROW_SETS - 1, 0, CHUNK)
        for m in range(ROW_SETS):
            f_part(0, m)
        for m in range(ROW_SETS):
            c_tilde_part(0, m)
            if m > 0:
                finish_c(0, m - 1)
        finish_c(0, ROW_SETS - 1)
        gates_done = [0]

        def gate_done():
            n = gates_done[0]
            if n % 2 == 0 and n // 2 < ROW_SETS:
                squash_c(0, n // 2)
            if n >= FIRST_TANH_1 and (n - FIRST_TANH_1) % 3 == 0 and (n - FIRST_TANH_1) // 3 < ROW_SETS:
                squash_c(1, (n - FIRST_TANH_1) // 3)
            gates_done[0] = n + 1

        for m in range(ROW_SETS):
            i_gates(1, m, 0, CHUNK)
            gate_done()
        for m in range(ROW_SETS):
            c_tilde_part(1, m)
            if m > 0:
                finish_c(1, m - 1)
            gate_done()
            f_part(1, m)
            gate_done()
        finish_c(1, ROW_SETS - 1)
        for m in range(ROW_SETS):
            o_part(0, m, (CHUNK,))
            gate_done()
        for m in range(ROW_SETS):
            o_part(1, m, LAST_WIDTHS[m])
            gate_done()
